import numpy as np
import ml_dtypes


def mxq(x, axis, fmt="e4m3"):
    dtype, down = {"e4m3": (ml_dtypes.float8_e4m3fn, 7), "e5m2": (ml_dtypes.float8_e5m2, 14)}[fmt]
    v = np.moveaxis(np.asarray(x, np.float32).astype(ml_dtypes.bfloat16).astype(np.float64), axis, -1)
    blocks = v.reshape(v.shape[:-1] + (-1, 32))
    amax = np.abs(blocks).max(-1, keepdims=True)
    byte = np.maximum(np.where(amax > 0, np.frexp(amax)[1] - 1 + 127, 0) - down, 1)
    scale = np.exp2(byte - 127.0)
    codes = (blocks / scale).astype(np.float32).astype(dtype).astype(np.float64)
    return np.moveaxis((codes * scale).reshape(v.shape), -1, axis)


WIDE = False


def mx_kscale(k):
    if not WIDE:
        return np.ones(k)
    levels = np.array([30, -30])
    if k % 512:
        return np.exp2(np.random.permutation(np.resize(levels, k // 32))).repeat(32)
    a = np.empty((k // 512, 16))
    for p in range(k // 512):
        a[p, :8] = np.random.permutation(np.resize(levels, 8))
        for g in range(8):
            far = levels[np.abs(levels - a[p, g]) >= 10]
            a[p, g + 8] = far[np.random.randint(len(far))]
    return np.exp2(a.ravel()).repeat(32)


BF16 = ml_dtypes.bfloat16


def bf(x):
    return np.asarray(x, np.float32).astype(BF16)


def f64(x):
    return np.asarray(x).astype(np.float64)


B, S, HID, NQ, NG, D, OFF = 1, 512, 2048, 16, 4, 128, 512
NKV = NQ // NG
HALF = D // 2


def rope(u, cos, sin):
    b, s, h, d = u.shape
    up = u.reshape(b, s, h, HALF, 2)
    ur, ui = up[..., 0], up[..., 1]
    c = cos[None, :, None, :]
    sn = sin[None, :, None, :]
    return np.stack([ur * c - ui * sn, ur * sn + ui * c], axis=-1).reshape(b, s, h, d)


def setup_inputs():
    sc = mx_kscale(HID)
    r = 1.0 / np.sqrt(HID)
    return {
        "x": bf(np.random.standard_normal((B, S, HID)) * sc),
        "precomp_freqs_cos": bf(np.random.uniform(-1.0, 1.0, (S, HALF))),
        "precomp_freqs_sin": bf(np.random.uniform(-1.0, 1.0, (S, HALF))),
        "q_w": bf(np.random.standard_normal((NQ * D, HID)) * 2.0 * r / sc),
        "q_b": bf(np.random.standard_normal(NQ * D) * 0.5),
        "k_w": bf(np.random.standard_normal((NKV * D, HID)) * 1.2 * r / sc),
        "k_b": bf(np.random.standard_normal(NKV * D) * 0.3),
        "v_w": bf(np.random.standard_normal((NKV * D, HID)) * r / sc),
        "v_b": bf(np.random.standard_normal(NKV * D) * 0.3),
    }


def reference(x, precomp_freqs_cos, precomp_freqs_sin, q_w, q_b, k_w, k_b, v_w, v_b):
    xq = mxq(f64(x), 2, "e5m2")
    q = ((xq @ mxq(f64(q_w), 1, "e5m2").T) + f64(q_b)).reshape(B, S, NQ, D)
    k = ((xq @ mxq(f64(k_w), 1, "e5m2").T) + f64(k_b)).reshape(B, S, NKV, D)
    v = ((xq @ mxq(f64(v_w), 1, "e5m2").T) + f64(v_b)).reshape(B, S, NKV, D)
    cos, sin = f64(precomp_freqs_cos), f64(precomp_freqs_sin)
    return rope(q, cos, sin), rope(k, cos, sin), v

@@ -1,0 +1,228 @@
+from contextlib import ExitStack
+
+import concourse.mybir as mybir
+from concourse.masks import make_identity
+
+FLOPS = 2 * 512 * 2048 * 3072
+
+F32 = mybir.dt.float32
+BF16 = mybir.dt.bfloat16
+U32 = mybir.dt.uint32
+U8 = mybir.dt.uint8
+FP8X4 = mybir.dt.float8_e5m2_x4
+ADD = mybir.AluOpType.add
+MULT = mybir.AluOpType.mult
+
+P = 128
+HID = 2048
+PASSES = 4
+BLOCK = 512
+HEADS = 4
+HALF = 64
+N_BLOCKS = 6
+
+
+def tile_attention_pa_kernel(
+    tc, x, precomp_freqs_cos, precomp_freqs_sin, q_w, q_b, k_w, k_b, v_w, v_b, out_0, out_1, out_2
+):
+    nc = tc.nc
+
+    def w_rows(b, r):
+        if b < 4:
+            return q_w[BLOCK * b + P * r : BLOCK * b + P * (r + 1), :]
+        if b == 4:
+            return k_w[P * r : P * (r + 1), :]
+        return v_w[P * r : P * (r + 1), :]
+
+    def out_rows(b, m):
+        rows = slice(P * m, P * (m + 1))
+        if b < 4:
+            return out_0[0, rows, HEADS * b : HEADS * (b + 1), :].rearrange("s h d -> s (h d)")
+        if b == 4:
+            return out_1[0, rows, :, :].rearrange("s h d -> s (h d)")
+        return out_2[0, rows, :, :].rearrange("s h d -> s (h d)")
+
+    with ExitStack() as ctx:
+        const = ctx.enter_context(tc.tile_pool(name="const", bufs=1))
+        rawp = ctx.enter_context(tc.tile_pool(name="rawp", bufs=16))
+        grpp = ctx.enter_context(tc.tile_pool(name="grpp", bufs=2))
+        codep = ctx.enter_context(tc.tile_pool(name="codep", bufs=2))
+        epp = ctx.enter_context(tc.tile_pool(name="epp", bufs=4))
+        tpp = ctx.enter_context(tc.psum_pool(name="tpp", bufs=4))
+        accp = ctx.enter_context(tc.psum_pool(name="accp", bufs=4))
+        ctx.enter_context(tc.manual_schedule())
+
+        def load(rows):
+            t = rawp.tile([P, HID], BF16, name="raw")
+            nc.sync.dma_start(out=t[:], in_=rows)
+            return t
+
+        def x_rows(m):
+            return x[0, P * m : P * (m + 1), :]
+
+        raw_w = {}
+        raw_x = {}
+        for r in range(4):
+            raw_w[(0, r)] = load(w_rows(0, r))
+        raw_x[0] = load(x_rows(0))
+        raw_x[1] = load(x_rows(1))
+        raw_w[(1, 0)] = load(w_rows(1, 0))
+        raw_w[(1, 1)] = load(w_rows(1, 1))
+        raw_x[2] = load(x_rows(2))
+        raw_x[3] = load(x_rows(3))
+        raw_w[(1, 2)] = load(w_rows(1, 2))
+        raw_w[(1, 3)] = load(w_rows(1, 3))
+        for r in range(4):
+            raw_w[(2, r)] = load(w_rows(2, r))
+
+        ident = const.tile([P, P], F32, name="ident")
+        make_identity(nc, ident[:])
+        ones = const.tile([P, P], BF16, name="ones")
+        nc.vector.memset(ones[:], 1.0)
+        brow = const.tile([P, N_BLOCKS * BLOCK], BF16, name="brow")
+        nc.vector.memset(brow[:].bitcast(F32), 0.0)
+        nc.scalar.dma_start(out=brow[0:1, 0:2048], in_=q_b.rearrange("(o n) -> o n", o=1))
+        nc.scalar.dma_start(out=brow[0:1, 2048:2560], in_=k_b.rearrange("(o n) -> o n", o=1))
+        nc.scalar.dma_start(out=brow[0:1, 2560:3072], in_=v_b.rearrange("(o n) -> o n", o=1))
+        cos_t = const.tile([P, 4, HALF], BF16, name="cos_t")
+        sin_t = const.tile([P, 4, HALF], BF16, name="sin_t")
+        nc.scalar.dma_start(out=cos_t[:], in_=precomp_freqs_cos.rearrange("(m p) j -> p m j", p=P))
+        nc.scalar.dma_start(out=sin_t[:], in_=precomp_freqs_sin.rearrange("(m p) j -> p m j", p=P))
+        cc = const.tile([P, 4, HALF, 2], BF16, name="cc")
+        nn = const.tile([P, 4, HALF, 2], BF16, name="nn")
+        nc.vector.tensor_copy(out=cc[:], in_=cos_t[:].unsqueeze(3).to_broadcast([P, 4, HALF, 2]))
+        nc.vector.tensor_scalar(out=nn[:, :, :, 0], in0=sin_t[:], scalar1=-1.0, scalar2=None, op0=MULT)
+        nc.vector.tensor_copy(out=nn[:, :, :, 1], in_=sin_t[:])
+
+        def transpose_rows(raw_t, dst):
+            words = raw_t[:].bitcast(F32)
+            for h in range(2):
+                tp = tpp.tile([P, 2, 2, P], F32, name="tp")
+                for gg in range(2):
+                    g = 2 * h + gg
+                    for u in range(2):
+                        nc.tensor.transpose(tp[:, gg, u, :], words[:, 256 * g + u : 256 * (g + 1) : 2], ident[:])
+                nc.scalar.copy(out=dst(h), in_=tp[:].rearrange("p g u r -> p g r u"))
+
+        x_codes = {}
+        x_scales = {}
+
+        def prep_x(m):
+            grp = grpp.tile([P, PASSES, P, 4], BF16, name="grpx", align_bytes=64)
+            gw = grp[:].bitcast(F32)
+            transpose_rows(raw_x[m], lambda h: gw[:, 2 * h : 2 * h + 2, :, :])
+            xc = const.tile([P, PASSES, P], U32, name="xc%d" % m, align_bytes=64)
+            xs = const.tile([P, PASSES, P], U8, name="xs%d" % m, align_bytes=64)
+            nc.vector.quantize_mx(
+                out=xc[:].rearrange("p g c -> p (g c)").bitcast(FP8X4),
+                scales=xs[:].rearrange("p g c -> p (g c)"),
+                in_=grp[:].rearrange("p g c t -> p (g c t)"),
+            )
+            x_codes[m] = xc
+            x_scales[m] = xs
+
+        grp_w = {}
+        w_codes = {}
+        w_scales = {}
+
+        def transpose_w(b, r):
+            if r == 0:
+                grp_w[b] = grpp.tile([P, PASSES, BLOCK, 4], BF16, name="grpw", align_bytes=64)
+            gw = grp_w[b][:].bitcast(F32)
+            transpose_rows(raw_w[(b, r)], lambda h: gw[:, 2 * h : 2 * h + 2, P * r : P * (r + 1), :])
+
+        def quantize_w(b, h):
+            if h == 0:
+                w_codes[b] = codep.tile([P, PASSES, BLOCK], U32, name="wc", align_bytes=64)
+                w_scales[b] = codep.tile([P, PASSES, BLOCK], U8, name="ws", align_bytes=64)
+            two = slice(2 * h, 2 * h + 2)
+            nc.vector.quantize_mx(
+                out=w_codes[b][:, two, :].rearrange("p g c -> p (g c)").bitcast(FP8X4),
+                scales=w_scales[b][:, two, :].rearrange("p g c -> p (g c)"),
+                in_=grp_w[b][:, two, :, :].rearrange("p g c t -> p (g c t)"),
+            )
+
+        bias_bc = {}
+
+        def bias_chunk(b):
+            ps = tpp.tile([P, BLOCK], F32, name="tp")
+            nc.tensor.matmul(out=ps[:], lhsT=ones[:], rhs=brow[:, BLOCK * b : BLOCK * (b + 1)], start=True, stop=True)
+            bias_bc[b] = const.tile([P, BLOCK], F32, name="bias%d" % b)
+            nc.scalar.copy(out=bias_bc[b][:], in_=ps[:])
+
+        def multiply(b, m):
+            acc = accp.tile([P, BLOCK], F32, name="acc")
+            for g in range(PASSES):
+                nc.tensor.matmul_mx(
+                    out=acc[:],
+                    lhsT=x_codes[m][:, g, :].bitcast(FP8X4),
+                    lhsT_scale=x_scales[m][:, g, :],
+                    rhs=w_codes[b][:, g, :].bitcast(FP8X4),
+                    rhs_scale=w_scales[b][:, g, :],
+                    start=(g == 0),
+                    stop=(g == PASSES - 1),
+                )
+            return acc
+
+        def epilogue_pair(b, ms, accs):
+            rope = b < 5
+            us = []
+            for acc in accs:
+                u = epp.tile([P, BLOCK], F32, name="u" if rope else "t1")
+                nc.vector.tensor_tensor(out=u[:], in0=acc[:], in1=bias_bc[b][:], op=ADD)
+                us.append(u)
+            res = us
+            if rope:
+                t1s = []
+                t2s = []
+                for m, u in zip(ms, us):
+                    t1 = epp.tile([P, BLOCK], F32, name="t1")
+                    nc.vector.tensor_tensor(
+                        out=t1[:].rearrange("p (h d) -> p h d", h=HEADS),
+                        in0=u[:].rearrange("p (h d) -> p h d", h=HEADS),
+                        in1=cc[:, m, :, :].rearrange("p j e -> p (j e)").unsqueeze(1).to_broadcast([P, HEADS, P]),
+                        op=MULT,
+                    )
+                    t1s.append(t1)
+                for m, u in zip(ms, us):
+                    t2 = epp.tile([P, BLOCK], F32, name="t2")
+                    nc.vector.tensor_tensor(
+                        out=t2[:].rearrange("p (h j e) -> p h j e", h=HEADS, e=2),
+                        in0=u[:].rearrange("p (h j e) -> p h j e", h=HEADS, e=2)[:, :, :, ::-1],
+                        in1=nn[:, m, :, :].unsqueeze(1).to_broadcast([P, HEADS, HALF, 2]),
+                        op=MULT,
+                    )
+                    t2s.append(t2)
+                for t1, t2 in zip(t1s, t2s):
+                    nc.vector.tensor_tensor(out=t1[:], in0=t1[:], in1=t2[:], op=ADD)
+                res = t1s
+            for m, t in zip(ms, res):
+                nc.sync.dma_start(out=out_rows(b, m), in_=t[:])
+                if b + 3 < N_BLOCKS:
+                    raw_w[(b + 3, m)] = load(w_rows(b + 3, m))
+
+        for r in range(4):
+            transpose_w(0, r)
+        quantize_w(0, 0)
+        prep_x(0)
+        quantize_w(0, 1)
+        bias_chunk(0)
+        prep_x(1)
+        for b in range(N_BLOCKS):
+            more = b + 1 < N_BLOCKS
+            if more:
+                transpose_w(b + 1, 0)
+                transpose_w(b + 1, 1)
+            accs = [multiply(b, 0), multiply(b, 1)]
+            epilogue_pair(b, (0, 1), accs)
+            if b == 0:
+                prep_x(2)
+                prep_x(3)
+            if more:
+                transpose_w(b + 1, 2)
+                transpose_w(b + 1, 3)
+                bias_chunk(b + 1)
+                quantize_w(b + 1, 0)
+                quantize_w(b + 1, 1)
+            accs = [multiply(b, 2), multiply(b, 3)]
+            epilogue_pair(b, (2, 3), accs)

@@ -164,15 +164,17 @@ def tile_attention_pa_kernel(
                 )
             return acc
 
-        def epilogue_pair(b, ms, accs):
-            rope = b < 5
+        def add_bias(b, accs):
             us = []
             for acc in accs:
-                u = epp.tile([P, BLOCK], F32, name="u" if rope else "t1")
+                u = epp.tile([P, BLOCK], F32, name="u" if b < 5 else "t1")
                 nc.vector.tensor_tensor(out=u[:], in0=acc[:], in1=bias_bc[b][:], op=ADD)
                 us.append(u)
+            return us
+
+        def rotate_and_store(b, ms, us):
             res = us
-            if rope:
+            if b < 5:
                 t1s = []
                 t2s = []
                 for m, u in zip(ms, us):
@@ -193,8 +195,8 @@ def tile_attention_pa_kernel(
                         op=MULT,
                     )
                     t2s.append(t2)
-                for t1, t2 in zip(t1s, t2s):
-                    nc.vector.tensor_tensor(out=t1[:], in0=t1[:], in1=t2[:], op=ADD)
+                nc.vector.tensor_tensor(out=t1s[0][:], in0=t1s[0][:], in1=t2s[0][:], op=ADD)
+                nc.gpsimd.tensor_tensor(out=t1s[1][:], in0=t1s[1][:], in1=t2s[1][:], op=ADD)
                 res = t1s
             for m, t in zip(ms, res):
                 nc.sync.dma_start(out=out_rows(b, m), in_=t[:])
@@ -213,8 +215,8 @@ def tile_attention_pa_kernel(
             if more:
                 transpose_w(b + 1, 0)
                 transpose_w(b + 1, 1)
-            accs = [multiply(b, 0), multiply(b, 1)]
-            epilogue_pair(b, (0, 1), accs)
+            us = add_bias(b, [multiply(b, 0), multiply(b, 1)])
+            rotate_and_store(b, (0, 1), us)
             if b == 0:
                 prep_x(2)
                 prep_x(3)
@@ -222,7 +224,8 @@ def tile_attention_pa_kernel(
                 transpose_w(b + 1, 2)
                 transpose_w(b + 1, 3)
                 bias_chunk(b + 1)
+            us = add_bias(b, [multiply(b, 2), multiply(b, 3)])
+            if more:
                 quantize_w(b + 1, 0)
                 quantize_w(b + 1, 1)
-            accs = [multiply(b, 2), multiply(b, 3)]
-            epilogue_pair(b, (2, 3), accs)
+            rotate_and_store(b, (2, 3), us)

@@ -20,6 +20,7 @@ BLOCK = 512
 HEADS = 4
 HALF = 64
 N_BLOCKS = 6
+FIRST_SORTED = 2
 
 
 def tile_attention_pa_kernel(
@@ -48,6 +49,7 @@ def tile_attention_pa_kernel(
         grpp = ctx.enter_context(tc.tile_pool(name="grpp", bufs=2))
         codep = ctx.enter_context(tc.tile_pool(name="codep", bufs=2))
         epp = ctx.enter_context(tc.tile_pool(name="epp", bufs=4))
+        rop = ctx.enter_context(tc.tile_pool(name="rop", bufs=4))
         tpp = ctx.enter_context(tc.psum_pool(name="tpp", bufs=4))
         accp = ctx.enter_context(tc.psum_pool(name="accp", bufs=4))
         ctx.enter_context(tc.manual_schedule())
@@ -94,15 +96,27 @@ def tile_attention_pa_kernel(
         nc.vector.tensor_scalar(out=nn[:, :, :, 0], in0=sin_t[:], scalar1=-1.0, scalar2=None, op0=MULT)
         nc.vector.tensor_copy(out=nn[:, :, :, 1], in_=sin_t[:])
 
-        def transpose_rows(raw_t, dst):
-            words = raw_t[:].bitcast(F32)
+        def transpose_rows(columns, dst):
             for h in range(2):
                 tp = tpp.tile([P, 2, 2, P], F32, name="tp")
                 for gg in range(2):
-                    g = 2 * h + gg
                     for u in range(2):
-                        nc.tensor.transpose(tp[:, gg, u, :], words[:, 256 * g + u : 256 * (g + 1) : 2], ident[:])
+                        nc.tensor.transpose(tp[:, gg, u, :], columns(2 * h + gg, u), ident[:])
                 nc.scalar.copy(out=dst(h), in_=tp[:].rearrange("p g u r -> p g r u"))
+
+        def every_second_word(raw_t):
+            words = raw_t[:].bitcast(F32)
+            return lambda g, u: words[:, 256 * g + u : 256 * (g + 1) : 2]
+
+        sorted_w = {}
+
+        def sort_words(b, r):
+            if FIRST_SORTED <= b < N_BLOCKS:
+                ro = rop.tile([P, PASSES, 2, P], F32, name="ro")
+                nc.scalar.copy(
+                    out=ro[:], in_=raw_w[(b, r)][:].bitcast(F32).rearrange("p (g w u) -> p g u w", g=PASSES, u=2)
+                )
+                sorted_w[(b, r)] = ro
 
         x_codes = {}
         x_scales = {}
@@ -110,7 +124,7 @@ def tile_attention_pa_kernel(
         def prep_x(m):
             grp = grpp.tile([P, PASSES, P, 4], BF16, name="grpx", align_bytes=64)
             gw = grp[:].bitcast(F32)
-            transpose_rows(raw_x[m], lambda h: gw[:, 2 * h : 2 * h + 2, :, :])
+            transpose_rows(every_second_word(raw_x[m]), lambda h: gw[:, 2 * h : 2 * h + 2, :, :])
             xc = const.tile([P, PASSES, P], U32, name="xc%d" % m, align_bytes=64)
             xs = const.tile([P, PASSES, P], U8, name="xs%d" % m, align_bytes=64)
             nc.vector.quantize_mx(
@@ -129,7 +143,12 @@ def tile_attention_pa_kernel(
             if r == 0:
                 grp_w[b] = grpp.tile([P, PASSES, BLOCK, 4], BF16, name="grpw", align_bytes=64)
             gw = grp_w[b][:].bitcast(F32)
-            transpose_rows(raw_w[(b, r)], lambda h: gw[:, 2 * h : 2 * h + 2, P * r : P * (r + 1), :])
+            if (b, r) in sorted_w:
+                ro = sorted_w[(b, r)]
+                columns = lambda g, u: ro[:, g, u, :]
+            else:
+                columns = every_second_word(raw_w[(b, r)])
+            transpose_rows(columns, lambda h: gw[:, 2 * h : 2 * h + 2, P * r : P * (r + 1), :])
 
         def quantize_w(b, h):
             if h == 0:
@@ -215,6 +234,8 @@ def tile_attention_pa_kernel(
             if more:
                 transpose_w(b + 1, 0)
                 transpose_w(b + 1, 1)
+                sort_words(b + 1, 2)
+                sort_words(b + 1, 3)
             us = add_bias(b, [multiply(b, 0), multiply(b, 1)])
             rotate_and_store(b, (0, 1), us)
             if b == 0:
@@ -224,6 +245,8 @@ def tile_attention_pa_kernel(
                 transpose_w(b + 1, 2)
                 transpose_w(b + 1, 3)
                 bias_chunk(b + 1)
+                sort_words(b + 2, 0)
+                sort_words(b + 2, 1)
             us = add_bias(b, [multiply(b, 2), multiply(b, 3)])
             if more:
                 quantize_w(b + 1, 0)

@@ -49,9 +49,11 @@ def tile_attention_pa_kernel(
         grpp = ctx.enter_context(tc.tile_pool(name="grpp", bufs=2))
         codep = ctx.enter_context(tc.tile_pool(name="codep", bufs=2))
         epp = ctx.enter_context(tc.tile_pool(name="epp", bufs=4))
+        outp = ctx.enter_context(tc.tile_pool(name="outp", bufs=6))
         rop = ctx.enter_context(tc.tile_pool(name="rop", bufs=4))
         tpp = ctx.enter_context(tc.psum_pool(name="tpp", bufs=4))
-        accp = ctx.enter_context(tc.psum_pool(name="accp", bufs=4))
+        accp = ctx.enter_context(tc.psum_pool(name="accp", bufs=3))
+        tabp = ctx.enter_context(tc.psum_pool(name="tabp", bufs=1))
         ctx.enter_context(tc.manual_schedule())
 
         def load(rows):
@@ -95,6 +97,20 @@ def tile_attention_pa_kernel(
         nc.vector.tensor_copy(out=cc[:], in_=cos_t[:].unsqueeze(3).to_broadcast([P, 4, HALF, 2]))
         nc.vector.tensor_scalar(out=nn[:, :, :, 0], in0=sin_t[:], scalar1=-1.0, scalar2=None, op0=MULT)
         nc.vector.tensor_copy(out=nn[:, :, :, 1], in_=sin_t[:])
+        ident_b = const.tile([P, P], BF16, name="ident_b")
+        make_identity(nc, ident_b[:])
+        tabs = tabp.tile([P, 2, 4, P], BF16, name="tabs")
+
+        def tables_to_psum():
+            for m in range(4):
+                for i, t in enumerate((cc, nn)):
+                    nc.tensor.matmul(
+                        out=tabs[:, i, m, :],
+                        lhsT=ident_b[:],
+                        rhs=t[:, m, :, :].rearrange("p j e -> p (j e)"),
+                        start=True,
+                        stop=True,
+                    )
 
         def transpose_rows(columns, dst):
             for h in range(2):
@@ -186,7 +202,7 @@ def tile_attention_pa_kernel(
         def add_bias(b, accs):
             us = []
             for acc in accs:
-                u = epp.tile([P, BLOCK], F32, name="u" if b < 5 else "t1")
+                u = epp.tile([P, BLOCK], F32, name="u")
                 nc.vector.tensor_tensor(out=u[:], in0=acc[:], in1=bias_bc[b][:], op=ADD)
                 us.append(u)
             return us
@@ -195,27 +211,23 @@ def tile_attention_pa_kernel(
             res = us
             if b < 5:
                 t1s = []
-                t2s = []
                 for m, u in zip(ms, us):
-                    t1 = epp.tile([P, BLOCK], F32, name="t1")
+                    t1 = outp.tile([P, BLOCK], F32, name="t1")
                     nc.vector.tensor_tensor(
                         out=t1[:].rearrange("p (h d) -> p h d", h=HEADS),
                         in0=u[:].rearrange("p (h d) -> p h d", h=HEADS),
-                        in1=cc[:, m, :, :].rearrange("p j e -> p (j e)").unsqueeze(1).to_broadcast([P, HEADS, P]),
+                        in1=tabs[:, 0, m, :].unsqueeze(1).to_broadcast([P, HEADS, P]),
                         op=MULT,
                     )
-                    t1s.append(t1)
-                for m, u in zip(ms, us):
                     t2 = epp.tile([P, BLOCK], F32, name="t2")
                     nc.vector.tensor_tensor(
                         out=t2[:].rearrange("p (h j e) -> p h j e", h=HEADS, e=2),
                         in0=u[:].rearrange("p (h j e) -> p h j e", h=HEADS, e=2)[:, :, :, ::-1],
-                        in1=nn[:, m, :, :].unsqueeze(1).to_broadcast([P, HEADS, HALF, 2]),
+                        in1=tabs[:, 1, m, :].rearrange("p (j e) -> p j e", e=2).unsqueeze(1).to_broadcast([P, HEADS, HALF, 2]),
                         op=MULT,
                     )
-                    t2s.append(t2)
-                nc.vector.tensor_tensor(out=t1s[0][:], in0=t1s[0][:], in1=t2s[0][:], op=ADD)
-                nc.gpsimd.tensor_tensor(out=t1s[1][:], in0=t1s[1][:], in1=t2s[1][:], op=ADD)
+                    nc.gpsimd.tensor_tensor(out=t1[:], in0=t1[:], in1=t2[:], op=ADD)
+                    t1s.append(t1)
                 res = t1s
             for m, t in zip(ms, res):
                 nc.sync.dma_start(out=out_rows(b, m), in_=t[:])
@@ -228,6 +240,7 @@ def tile_attention_pa_kernel(
         prep_x(0)
         quantize_w(0, 1)
         bias_chunk(0)
+        tables_to_psum()
         prep_x(1)
         for b in range(N_BLOCKS):
             more = b + 1 < N_BLOCKS

@@ -185,19 +185,26 @@ def tile_attention_pa_kernel(
             bias_bc[b] = const.tile([P, BLOCK], F32, name="bias%d" % b)
             nc.scalar.copy(out=bias_bc[b][:], in_=ps[:])
 
-        def multiply(b, m):
-            acc = accp.tile([P, BLOCK], F32, name="acc")
-            for g in range(PASSES):
+        def multiply_pair(b, ms):
+            accs = []
+            for m in ms:
+                acc = accp.tile([P, BLOCK], F32, name="acc")
+                accs.append(acc)
+            if ms[0] == 0:
+                order = [(i, g) for h in range(2) for i in range(2) for g in (2 * h, 2 * h + 1)]
+            else:
+                order = [(i, g) for i in range(2) for g in range(PASSES)]
+            for i, g in order:
                 nc.tensor.matmul_mx(
-                    out=acc[:],
-                    lhsT=x_codes[m][:, g, :].bitcast(FP8X4),
-                    lhsT_scale=x_scales[m][:, g, :],
+                    out=accs[i][:],
+                    lhsT=x_codes[ms[i]][:, g, :].bitcast(FP8X4),
+                    lhsT_scale=x_scales[ms[i]][:, g, :],
                     rhs=w_codes[b][:, g, :].bitcast(FP8X4),
                     rhs_scale=w_scales[b][:, g, :],
                     start=(g == 0),
                     stop=(g == PASSES - 1),
                 )
-            return acc
+            return accs
 
         def add_bias(b, accs):
             us = []
@@ -230,7 +237,8 @@ def tile_attention_pa_kernel(
                     t1s.append(t1)
                 res = t1s
             for m, t in zip(ms, res):
-                nc.sync.dma_start(out=out_rows(b, m), in_=t[:])
+                queue = nc.sync if b < 5 else nc.scalar
+                queue.dma_start(out=out_rows(b, m), in_=t[:])
                 if b + 3 < N_BLOCKS:
                     raw_w[(b + 3, m)] = load(w_rows(b + 3, m))
 
@@ -249,7 +257,7 @@ def tile_attention_pa_kernel(
                 transpose_w(b + 1, 1)
                 sort_words(b + 1, 2)
                 sort_words(b + 1, 3)
-            us = add_bias(b, [multiply(b, 0), multiply(b, 1)])
+            us = add_bias(b, multiply_pair(b, (0, 1)))
             rotate_and_store(b, (0, 1), us)
             if b == 0:
                 prep_x(2)
@@ -260,7 +268,7 @@ def tile_attention_pa_kernel(
                 bias_chunk(b + 1)
                 sort_words(b + 2, 0)
                 sort_words(b + 2, 1)
-            us = add_bias(b, [multiply(b, 2), multiply(b, 3)])
+            us = add_bias(b, multiply_pair(b, (2, 3)))
             if more:
                 quantize_w(b + 1, 0)
                 quantize_w(b + 1, 1)

@@ -137,10 +137,24 @@ def tile_attention_pa_kernel(
         x_codes = {}
         x_scales = {}
 
+        sorted_x = {}
+
+        def sort_x_words(m):
+            ro = rop.tile([P, PASSES, 2, P], F32, name="rox")
+            nc.vector.tensor_copy(
+                out=ro[:], in_=raw_x[m][:].bitcast(F32).rearrange("p (g w u) -> p g u w", g=PASSES, u=2)
+            )
+            sorted_x[m] = ro
+
         def prep_x(m):
             grp = grpp.tile([P, PASSES, P, 4], BF16, name="grpx", align_bytes=64)
             gw = grp[:].bitcast(F32)
-            transpose_rows(every_second_word(raw_x[m]), lambda h: gw[:, 2 * h : 2 * h + 2, :, :])
+            if m in sorted_x:
+                ro = sorted_x[m]
+                columns = lambda g, u: ro[:, g, u, :]
+            else:
+                columns = every_second_word(raw_x[m])
+            transpose_rows(columns, lambda h: gw[:, 2 * h : 2 * h + 2, :, :])
             xc = const.tile([P, PASSES, P], U32, name="xc%d" % m, align_bytes=64)
             xs = const.tile([P, PASSES, P], U8, name="xs%d" % m, align_bytes=64)
             nc.vector.quantize_mx(
@@ -250,6 +264,8 @@ def tile_attention_pa_kernel(
         bias_chunk(0)
         tables_to_psum()
         prep_x(1)
+        sort_x_words(2)
+        sort_x_words(3)
         for b in range(N_BLOCKS):
             more = b + 1 < N_BLOCKS
             if more:

@@ -284,8 +284,9 @@ def tile_attention_pa_kernel(
                 bias_chunk(b + 1)
                 sort_words(b + 2, 0)
                 sort_words(b + 2, 1)
-            us = add_bias(b, multiply_pair(b, (2, 3)))
+            accs = multiply_pair(b, (2, 3))
             if more:
                 quantize_w(b + 1, 0)
                 quantize_w(b + 1, 1)
+            us = add_bias(b, accs)
             rotate_and_store(b, (2, 3), us)

@@ -232,14 +232,27 @@ def tile_attention_pa_kernel(
             res = us
             if b < 5:
                 t1s = []
-                for m, u in zip(ms, us):
+                first = {}
+                if ms[1] == 3:
                     t1 = outp.tile([P, BLOCK], F32, name="t1")
-                    nc.vector.tensor_tensor(
+                    nc.gpsimd.tensor_tensor(
                         out=t1[:].rearrange("p (h d) -> p h d", h=HEADS),
-                        in0=u[:].rearrange("p (h d) -> p h d", h=HEADS),
-                        in1=tabs[:, 0, m, :].unsqueeze(1).to_broadcast([P, HEADS, P]),
+                        in0=us[1][:].rearrange("p (h d) -> p h d", h=HEADS),
+                        in1=cc[:, 3, :, :].rearrange("p j e -> p (j e)").unsqueeze(1).to_broadcast([P, HEADS, P]),
                         op=MULT,
                     )
+                    first[3] = t1
+                for m, u in zip(ms, us):
+                    if m in first:
+                        t1 = first[m]
+                    else:
+                        t1 = outp.tile([P, BLOCK], F32, name="t1")
+                        nc.vector.tensor_tensor(
+                            out=t1[:].rearrange("p (h d) -> p h d", h=HEADS),
+                            in0=u[:].rearrange("p (h d) -> p h d", h=HEADS),
+                            in1=tabs[:, 0, m, :].unsqueeze(1).to_broadcast([P, HEADS, P]),
+                            op=MULT,
+                        )
                     t2 = epp.tile([P, BLOCK], F32, name="t2")
                     nc.vector.tensor_tensor(
                         out=t2[:].rearrange("p (h j e) -> p h j e", h=HEADS, e=2),

@@ -21,6 +21,7 @@ HEADS = 4
 HALF = 64
 N_BLOCKS = 6
 FIRST_SORTED = 2
+SORTED_ROW_TILES = (1, 2, 3)
 
 
 def tile_attention_pa_kernel(
@@ -50,7 +51,7 @@ def tile_attention_pa_kernel(
         codep = ctx.enter_context(tc.tile_pool(name="codep", bufs=2))
         epp = ctx.enter_context(tc.tile_pool(name="epp", bufs=4))
         outp = ctx.enter_context(tc.tile_pool(name="outp", bufs=6))
-        rop = ctx.enter_context(tc.tile_pool(name="rop", bufs=4))
+        rop = ctx.enter_context(tc.tile_pool(name="rop", bufs=6))
         tpp = ctx.enter_context(tc.psum_pool(name="tpp", bufs=4))
         accp = ctx.enter_context(tc.psum_pool(name="accp", bufs=3))
         tabp = ctx.enter_context(tc.psum_pool(name="tabp", bufs=1))
@@ -127,7 +128,7 @@ def tile_attention_pa_kernel(
         sorted_w = {}
 
         def sort_words(b, r):
-            if FIRST_SORTED <= b < N_BLOCKS:
+            if FIRST_SORTED <= b < N_BLOCKS and r in SORTED_ROW_TILES:
                 ro = rop.tile([P, PASSES, 2, P], F32, name="ro")
                 nc.scalar.copy(
                     out=ro[:], in_=raw_w[(b, r)][:].bitcast(F32).rearrange("p (g w u) -> p g u w", g=PASSES, u=2)
@@ -284,7 +285,6 @@ def tile_attention_pa_kernel(
             if more:
                 transpose_w(b + 1, 0)
                 transpose_w(b + 1, 1)
-                sort_words(b + 1, 2)
                 sort_words(b + 1, 3)
             us = add_bias(b, multiply_pair(b, (0, 1)))
             rotate_and_store(b, (0, 1), us)
@@ -295,8 +295,8 @@ def tile_attention_pa_kernel(
                 transpose_w(b + 1, 2)
                 transpose_w(b + 1, 3)
                 bias_chunk(b + 1)
-                sort_words(b + 2, 0)
                 sort_words(b + 2, 1)
+                sort_words(b + 2, 2)
             accs = multiply_pair(b, (2, 3))
             if more:
                 quantize_w(b + 1, 0)

@@ -20,6 +20,7 @@ BLOCK = 512
 HEADS = 4
 HALF = 64
 N_BLOCKS = 6
+V_BLOCK = 5
 FIRST_SORTED = 2
 SORTED_ROW_TILES = (1, 2, 3)
 
@@ -65,6 +66,19 @@ def tile_attention_pa_kernel(
         def x_rows(m):
             return x[0, P * m : P * (m + 1), :]
 
+        cos_t = const.tile([P, 4, HALF], BF16, name="cos_t")
+        sin_t = const.tile([P, 4, HALF], BF16, name="sin_t")
+        nc.scalar.dma_start(out=cos_t[:], in_=precomp_freqs_cos.rearrange("(m p) j -> p m j", p=P))
+        nc.scalar.dma_start(out=sin_t[:], in_=precomp_freqs_sin.rearrange("(m p) j -> p m j", p=P))
+        brow = const.tile([P, BLOCK], BF16, name="brow")
+        nc.vector.memset(brow[:].bitcast(F32), 0.0)
+        nc.scalar.dma_start(out=brow[0:4, :], in_=q_b.rearrange("(o n) -> o n", o=4))
+        nc.scalar.dma_start(out=brow[4:5, :], in_=k_b.rearrange("(o n) -> o n", o=1))
+        nc.scalar.dma_start(out=brow[5:6, :], in_=v_b.rearrange("(o n) -> o n", o=1))
+        warm = const.tile([P, 2], F32, name="warm")
+        nc.vector.memset(warm[:, 0:1], 0.0)
+        nc.scalar.copy(out=warm[:, 1:2], in_=warm[:, 0:1])
+
         raw_w = {}
         raw_x = {}
         for r in range(4):
@@ -82,17 +96,6 @@ def tile_attention_pa_kernel(
 
         ident = const.tile([P, P], F32, name="ident")
         make_identity(nc, ident[:])
-        ones = const.tile([P, P], BF16, name="ones")
-        nc.vector.memset(ones[:], 1.0)
-        brow = const.tile([P, N_BLOCKS * BLOCK], BF16, name="brow")
-        nc.vector.memset(brow[:].bitcast(F32), 0.0)
-        nc.scalar.dma_start(out=brow[0:1, 0:2048], in_=q_b.rearrange("(o n) -> o n", o=1))
-        nc.scalar.dma_start(out=brow[0:1, 2048:2560], in_=k_b.rearrange("(o n) -> o n", o=1))
-        nc.scalar.dma_start(out=brow[0:1, 2560:3072], in_=v_b.rearrange("(o n) -> o n", o=1))
-        cos_t = const.tile([P, 4, HALF], BF16, name="cos_t")
-        sin_t = const.tile([P, 4, HALF], BF16, name="sin_t")
-        nc.scalar.dma_start(out=cos_t[:], in_=precomp_freqs_cos.rearrange("(m p) j -> p m j", p=P))
-        nc.scalar.dma_start(out=sin_t[:], in_=precomp_freqs_sin.rearrange("(m p) j -> p m j", p=P))
         cc = const.tile([P, 4, HALF, 2], BF16, name="cc")
         nn = const.tile([P, 4, HALF, 2], BF16, name="nn")
         nc.vector.tensor_copy(out=cc[:], in_=cos_t[:].unsqueeze(3).to_broadcast([P, 4, HALF, 2]))
@@ -147,7 +150,9 @@ def tile_attention_pa_kernel(
             )
             sorted_x[m] = ro
 
-        def prep_x(m):
+        grp_x = {}
+
+        def transpose_x(m):
             grp = grpp.tile([P, PASSES, P, 4], BF16, name="grpx", align_bytes=64)
             gw = grp[:].bitcast(F32)
             if m in sorted_x:
@@ -156,12 +161,15 @@ def tile_attention_pa_kernel(
             else:
                 columns = every_second_word(raw_x[m])
             transpose_rows(columns, lambda h: gw[:, 2 * h : 2 * h + 2, :, :])
+            grp_x[m] = grp
+
+        def quantize_x(m):
             xc = const.tile([P, PASSES, P], U32, name="xc%d" % m, align_bytes=64)
             xs = const.tile([P, PASSES, P], U8, name="xs%d" % m, align_bytes=64)
             nc.vector.quantize_mx(
                 out=xc[:].rearrange("p g c -> p (g c)").bitcast(FP8X4),
                 scales=xs[:].rearrange("p g c -> p (g c)"),
-                in_=grp[:].rearrange("p g c t -> p (g c t)"),
+                in_=grp_x[m][:].rearrange("p g c t -> p (g c t)"),
             )
             x_codes[m] = xc
             x_scales[m] = xs
@@ -181,10 +189,24 @@ def tile_attention_pa_kernel(
                 columns = every_second_word(raw_w[(b, r)])
             transpose_rows(columns, lambda h: gw[:, 2 * h : 2 * h + 2, P * r : P * (r + 1), :])
 
+        def w_code_tiles(b):
+            w_codes[b] = codep.tile([P, PASSES, BLOCK], U32, name="wc", align_bytes=64)
+            w_scales[b] = codep.tile([P, PASSES, BLOCK], U8, name="ws", align_bytes=64)
+
+        def quantize_w_rows(b, r):
+            if r == 0:
+                w_code_tiles(b)
+            cols = slice(P * r, P * (r + 1))
+            for g in range(PASSES):
+                nc.vector.quantize_mx(
+                    out=w_codes[b][:, g, cols].bitcast(FP8X4),
+                    scales=w_scales[b][:, g, cols],
+                    in_=grp_w[b][:, g, cols, :].rearrange("p c t -> p (c t)"),
+                )
+
         def quantize_w(b, h):
             if h == 0:
-                w_codes[b] = codep.tile([P, PASSES, BLOCK], U32, name="wc", align_bytes=64)
-                w_scales[b] = codep.tile([P, PASSES, BLOCK], U8, name="ws", align_bytes=64)
+                w_code_tiles(b)
             two = slice(2 * h, 2 * h + 2)
             nc.vector.quantize_mx(
                 out=w_codes[b][:, two, :].rearrange("p g c -> p (g c)").bitcast(FP8X4),
@@ -196,30 +218,25 @@ def tile_attention_pa_kernel(
 
         def bias_chunk(b):
             ps = tpp.tile([P, BLOCK], F32, name="tp")
-            nc.tensor.matmul(out=ps[:], lhsT=ones[:], rhs=brow[:, BLOCK * b : BLOCK * (b + 1)], start=True, stop=True)
+            nc.tensor.matmul(
+                out=ps[:], lhsT=ident_b[:, b : b + 1].to_broadcast([P, P]), rhs=brow[:], start=True, stop=True
+            )
             bias_bc[b] = const.tile([P, BLOCK], F32, name="bias%d" % b)
             nc.scalar.copy(out=bias_bc[b][:], in_=ps[:])
 
-        def multiply_pair(b, ms):
-            accs = []
-            for m in ms:
-                acc = accp.tile([P, BLOCK], F32, name="acc")
-                accs.append(acc)
-            if ms[0] == 0:
-                order = [(i, g) for h in range(2) for i in range(2) for g in (2 * h, 2 * h + 1)]
-            else:
-                order = [(i, g) for i in range(2) for g in range(PASSES)]
-            for i, g in order:
+        def multiply(b, m):
+            acc = accp.tile([P, BLOCK], F32, name="acc")
+            for g in range(PASSES):
                 nc.tensor.matmul_mx(
-                    out=accs[i][:],
-                    lhsT=x_codes[ms[i]][:, g, :].bitcast(FP8X4),
-                    lhsT_scale=x_scales[ms[i]][:, g, :],
+                    out=acc[:],
+                    lhsT=x_codes[m][:, g, :].bitcast(FP8X4),
+                    lhsT_scale=x_scales[m][:, g, :],
                     rhs=w_codes[b][:, g, :].bitcast(FP8X4),
                     rhs_scale=w_scales[b][:, g, :],
                     start=(g == 0),
                     stop=(g == PASSES - 1),
                 )
-            return accs
+            return acc
 
         def add_bias(b, accs):
             us = []
@@ -229,77 +246,103 @@ def tile_attention_pa_kernel(
                 us.append(u)
             return us
 
-        def rotate_and_store(b, ms, us):
-            res = us
-            if b < 5:
-                t1s = []
-                first = {}
-                if ms[1] == 3:
-                    t1 = outp.tile([P, BLOCK], F32, name="t1")
-                    nc.gpsimd.tensor_tensor(
-                        out=t1[:].rearrange("p (h d) -> p h d", h=HEADS),
-                        in0=us[1][:].rearrange("p (h d) -> p h d", h=HEADS),
-                        in1=cc[:, 3, :, :].rearrange("p j e -> p (j e)").unsqueeze(1).to_broadcast([P, HEADS, P]),
-                        op=MULT,
-                    )
-                    first[3] = t1
-                for m, u in zip(ms, us):
-                    if m in first:
-                        t1 = first[m]
-                    else:
-                        t1 = outp.tile([P, BLOCK], F32, name="t1")
-                        nc.vector.tensor_tensor(
-                            out=t1[:].rearrange("p (h d) -> p h d", h=HEADS),
-                            in0=u[:].rearrange("p (h d) -> p h d", h=HEADS),
-                            in1=tabs[:, 0, m, :].unsqueeze(1).to_broadcast([P, HEADS, P]),
-                            op=MULT,
-                        )
-                    t2 = epp.tile([P, BLOCK], F32, name="t2")
+        def add_bias_and_store_v(ms, accs):
+            for m, acc in zip(ms, accs):
+                u = epp.tile([P, BLOCK], F32, name="u")
+                pieces = 2 if m == 3 else 1
+                width = BLOCK // pieces
+                for i in range(pieces):
+                    cols = slice(width * i, width * (i + 1))
                     nc.vector.tensor_tensor(
-                        out=t2[:].rearrange("p (h j e) -> p h j e", h=HEADS, e=2),
-                        in0=u[:].rearrange("p (h j e) -> p h j e", h=HEADS, e=2)[:, :, :, ::-1],
-                        in1=tabs[:, 1, m, :].rearrange("p (j e) -> p j e", e=2).unsqueeze(1).to_broadcast([P, HEADS, HALF, 2]),
+                        out=u[:, cols], in0=acc[:, cols], in1=bias_bc[V_BLOCK][:, cols], op=ADD
+                    )
+                    nc.scalar.dma_start(out=out_rows(V_BLOCK, m)[:, cols], in_=u[:, cols])
+
+        def rotate_and_store(b, ms, us):
+            t1s = []
+            first = {}
+            if ms[-1] == 3:
+                t1 = outp.tile([P, BLOCK], F32, name="t1")
+                nc.gpsimd.tensor_tensor(
+                    out=t1[:].rearrange("p (h d) -> p h d", h=HEADS),
+                    in0=us[-1][:].rearrange("p (h d) -> p h d", h=HEADS),
+                    in1=cc[:, 3, :, :].rearrange("p j e -> p (j e)").unsqueeze(1).to_broadcast([P, HEADS, P]),
+                    op=MULT,
+                )
+                first[3] = t1
+            for m, u in zip(ms, us):
+                if m in first:
+                    t1 = first[m]
+                else:
+                    t1 = outp.tile([P, BLOCK], F32, name="t1")
+                    nc.vector.tensor_tensor(
+                        out=t1[:].rearrange("p (h d) -> p h d", h=HEADS),
+                        in0=u[:].rearrange("p (h d) -> p h d", h=HEADS),
+                        in1=tabs[:, 0, m, :].unsqueeze(1).to_broadcast([P, HEADS, P]),
                         op=MULT,
                     )
-                    nc.gpsimd.tensor_tensor(out=t1[:], in0=t1[:], in1=t2[:], op=ADD)
-                    t1s.append(t1)
-                res = t1s
-            for m, t in zip(ms, res):
-                queue = nc.sync if b < 5 else nc.scalar
-                queue.dma_start(out=out_rows(b, m), in_=t[:])
+                t2 = epp.tile([P, BLOCK], F32, name="t2")
+                nc.vector.tensor_tensor(
+                    out=t2[:].rearrange("p (h j e) -> p h j e", h=HEADS, e=2),
+                    in0=u[:].rearrange("p (h j e) -> p h j e", h=HEADS, e=2)[:, :, :, ::-1],
+                    in1=tabs[:, 1, m, :].rearrange("p (j e) -> p j e", e=2).unsqueeze(1).to_broadcast([P, HEADS, HALF, 2]),
+                    op=MULT,
+                )
+                nc.gpsimd.tensor_tensor(out=t1[:], in0=t1[:], in1=t2[:], op=ADD)
+                t1s.append(t1)
+            for m, t in zip(ms, t1s):
+                nc.sync.dma_start(out=out_rows(b, m), in_=t[:])
                 if b + 3 < N_BLOCKS:
                     raw_w[(b + 3, m)] = load(w_rows(b + 3, m))
 
         for r in range(4):
             transpose_w(0, r)
-        quantize_w(0, 0)
-        prep_x(0)
-        quantize_w(0, 1)
+            if r > 0:
+                quantize_w_rows(0, r - 1)
+        quantize_w_rows(0, 3)
+        transpose_x(0)
         bias_chunk(0)
         tables_to_psum()
-        prep_x(1)
+        transpose_x(1)
+        quantize_x(0)
+        quantize_x(1)
         sort_x_words(2)
         sort_x_words(3)
         for b in range(N_BLOCKS):
             more = b + 1 < N_BLOCKS
-            if more:
-                transpose_w(b + 1, 0)
-                transpose_w(b + 1, 1)
-                sort_words(b + 1, 3)
-            us = add_bias(b, multiply_pair(b, (0, 1)))
-            rotate_and_store(b, (0, 1), us)
             if b == 0:
-                prep_x(2)
-                prep_x(3)
+                transpose_w(1, 0)
+                us = add_bias(0, [multiply(0, 0)])
+                transpose_w(1, 1)
+                transpose_x(2)
+                acc = multiply(0, 1)
+                rotate_and_store(0, (0,), us)
+                us = add_bias(0, [acc])
+                transpose_x(3)
+                quantize_x(2)
+                rotate_and_store(0, (1,), us)
+                quantize_x(3)
+            else:
+                if more:
+                    transpose_w(b + 1, 0)
+                    transpose_w(b + 1, 1)
+                    sort_words(b + 1, 3)
+                accs = [multiply(b, 0), multiply(b, 1)]
+                if b == V_BLOCK:
+                    add_bias_and_store_v((0, 1), accs)
+                else:
+                    rotate_and_store(b, (0, 1), add_bias(b, accs))
             if more:
                 transpose_w(b + 1, 2)
                 transpose_w(b + 1, 3)
                 bias_chunk(b + 1)
                 sort_words(b + 2, 1)
                 sort_words(b + 2, 2)
-            accs = multiply_pair(b, (2, 3))
+            accs = [multiply(b, 2), multiply(b, 3)]
             if more:
                 quantize_w(b + 1, 0)
                 quantize_w(b + 1, 1)
-            us = add_bias(b, accs)
-            rotate_and_store(b, (2, 3), us)
+            if b == V_BLOCK:
+                add_bias_and_store_v((2, 3), accs)
+            else:
+                rotate_and_store(b, (2, 3), add_bias(b, accs))

@@ -50,8 +50,8 @@ def tile_attention_pa_kernel(
         rawp = ctx.enter_context(tc.tile_pool(name="rawp", bufs=16))
         grpp = ctx.enter_context(tc.tile_pool(name="grpp", bufs=2))
         codep = ctx.enter_context(tc.tile_pool(name="codep", bufs=2))
-        epp = ctx.enter_context(tc.tile_pool(name="epp", bufs=4))
-        outp = ctx.enter_context(tc.tile_pool(name="outp", bufs=6))
+        epp = ctx.enter_context(tc.tile_pool(name="epp", bufs=2))
+        outp = ctx.enter_context(tc.tile_pool(name="outp", bufs=3))
         rop = ctx.enter_context(tc.tile_pool(name="rop", bufs=6))
         tpp = ctx.enter_context(tc.psum_pool(name="tpp", bufs=4))
         accp = ctx.enter_context(tc.psum_pool(name="accp", bufs=3))
@@ -238,71 +238,109 @@ def tile_attention_pa_kernel(
                 )
             return acc
 
-        def add_bias(b, accs):
-            us = []
-            for acc in accs:
-                u = epp.tile([P, BLOCK], F32, name="u")
-                nc.vector.tensor_tensor(out=u[:], in0=acc[:], in1=bias_bc[b][:], op=ADD)
-                us.append(u)
-            return us
+        biased = {}
+        by_cos = {}
+        by_sin = {}
 
-        def add_bias_and_store_v(ms, accs):
-            for m, acc in zip(ms, accs):
-                u = epp.tile([P, BLOCK], F32, name="u")
-                pieces = 2 if m == 3 else 1
-                width = BLOCK // pieces
-                for i in range(pieces):
-                    cols = slice(width * i, width * (i + 1))
-                    nc.vector.tensor_tensor(
-                        out=u[:, cols], in0=acc[:, cols], in1=bias_bc[V_BLOCK][:, cols], op=ADD
-                    )
-                    nc.scalar.dma_start(out=out_rows(V_BLOCK, m)[:, cols], in_=u[:, cols])
+        def half_of_pair(tiles, pool, tag, b, m):
+            key = (b, m // 2)
+            if key not in tiles:
+                t = pool.tile([P, 2, BLOCK], F32, name=tag)
+                tiles[key] = t
+            return tiles[key][:, m % 2, :]
 
-        def rotate_and_store(b, ms, us):
-            t1s = []
-            first = {}
-            if ms[-1] == 3:
-                t1 = outp.tile([P, BLOCK], F32, name="t1")
-                nc.gpsimd.tensor_tensor(
-                    out=t1[:].rearrange("p (h d) -> p h d", h=HEADS),
-                    in0=us[-1][:].rearrange("p (h d) -> p h d", h=HEADS),
-                    in1=cc[:, 3, :, :].rearrange("p j e -> p (j e)").unsqueeze(1).to_broadcast([P, HEADS, P]),
-                    op=MULT,
-                )
-                first[3] = t1
-            for m, u in zip(ms, us):
-                if m in first:
-                    t1 = first[m]
-                else:
-                    t1 = outp.tile([P, BLOCK], F32, name="t1")
-                    nc.vector.tensor_tensor(
-                        out=t1[:].rearrange("p (h d) -> p h d", h=HEADS),
-                        in0=u[:].rearrange("p (h d) -> p h d", h=HEADS),
-                        in1=tabs[:, 0, m, :].unsqueeze(1).to_broadcast([P, HEADS, P]),
-                        op=MULT,
-                    )
-                t2 = epp.tile([P, BLOCK], F32, name="t2")
-                nc.vector.tensor_tensor(
-                    out=t2[:].rearrange("p (h j e) -> p h j e", h=HEADS, e=2),
-                    in0=u[:].rearrange("p (h j e) -> p h j e", h=HEADS, e=2)[:, :, :, ::-1],
-                    in1=tabs[:, 1, m, :].rearrange("p (j e) -> p j e", e=2).unsqueeze(1).to_broadcast([P, HEADS, HALF, 2]),
-                    op=MULT,
-                )
-                nc.gpsimd.tensor_tensor(out=t1[:], in0=t1[:], in1=t2[:], op=ADD)
-                t1s.append(t1)
-            for m, t in zip(ms, t1s):
-                nc.sync.dma_start(out=out_rows(b, m), in_=t[:])
-                if b + 3 < N_BLOCKS:
-                    raw_w[(b + 3, m)] = load(w_rows(b + 3, m))
+        def add_bias(b, m, acc, cols):
+            u = half_of_pair(biased, epp, "u", b, m)
+            nc.vector.tensor_tensor(out=u[:, cols], in0=acc[:, cols], in1=bias_bc[b][:, cols], op=ADD)
 
-        for r in range(4):
-            transpose_w(0, r)
-            if r > 0:
-                quantize_w_rows(0, r - 1)
-        quantize_w_rows(0, 3)
-        transpose_x(0)
+        def multiply_by_cos(engine, table, b, m):
+            t1 = half_of_pair(by_cos, outp, "t1", b, m)
+            u = half_of_pair(biased, epp, "u", b, m)
+            engine.tensor_tensor(
+                out=t1.rearrange("p (h d) -> p h d", h=HEADS),
+                in0=u.rearrange("p (h d) -> p h d", h=HEADS),
+                in1=table.unsqueeze(1).to_broadcast([P, HEADS, P]),
+                op=MULT,
+            )
+
+        def multiply_by_cos_on_vector(b, m):
+            multiply_by_cos(nc.vector, tabs[:, 0, m, :], b, m)
+
+        def multiply_by_cos_on_gpsimd(b, m):
+            multiply_by_cos(nc.gpsimd, cc[:, m, :, :].rearrange("p j e -> p (j e)"), b, m)
+
+        def multiply_by_sin(b, m):
+            t2 = half_of_pair(by_sin, epp, "t2", b, m)
+            u = half_of_pair(biased, epp, "u", b, m)
+            nc.vector.tensor_tensor(
+                out=t2.rearrange("p (h j e) -> p h j e", h=HEADS, e=2),
+                in0=u.rearrange("p (h j e) -> p h j e", h=HEADS, e=2)[:, :, :, ::-1],
+                in1=tabs[:, 1, m, :].rearrange("p (j e) -> p j e", e=2).unsqueeze(1).to_broadcast([P, HEADS, HALF, 2]),
+                op=MULT,
+            )
+
+        def add_products(b, ms):
+            some = slice(ms[0] % 2, ms[0] % 2 + len(ms))
+            t1 = by_cos[(b, ms[0] // 2)][:, some, :]
+            t2 = by_sin[(b, ms[0] // 2)][:, some, :]
+            nc.gpsimd.tensor_tensor(out=t1, in0=t1, in1=t2, op=ADD)
+
+        def store(b, ms):
+            for m in ms:
+                nc.sync.dma_start(out=out_rows(b, m), in_=half_of_pair(by_cos, outp, "t1", b, m))
+
+        def rotate_single(b, m):
+            multiply_by_cos_on_vector(b, m)
+            multiply_by_sin(b, m)
+            add_products(b, (m,))
+            store(b, (m,))
+
+        def rotate_first_pair(b):
+            multiply_by_cos_on_gpsimd(b, 1)
+            multiply_by_cos_on_vector(b, 0)
+            multiply_by_sin(b, 0)
+            multiply_by_sin(b, 1)
+            add_products(b, (0, 1))
+            store(b, (0, 1))
+
+        def rotate_second_pair(b):
+            if b == 0:
+                multiply_by_cos_on_gpsimd(b, 3)
+            multiply_by_cos_on_vector(b, 2)
+            multiply_by_sin(b, 2)
+            add_products(b, (2,))
+            if b > 0:
+                multiply_by_cos_on_vector(b, 3)
+            multiply_by_sin(b, 3)
+            add_products(b, (3,))
+            store(b, (2, 3))
+
+        def add_bias_and_store_v(m, acc):
+            pieces = 2 if m == 3 else 1
+            width = BLOCK // pieces
+            for i in range(pieces):
+                cols = slice(width * i, width * (i + 1))
+                add_bias(V_BLOCK, m, acc, cols)
+                u = half_of_pair(biased, epp, "u", V_BLOCK, m)
+                nc.scalar.dma_start(out=out_rows(V_BLOCK, m)[:, cols], in_=u[:, cols])
+
+        def load_block(b):
+            if b < N_BLOCKS:
+                for r in range(4):
+                    raw_w[(b, r)] = load(w_rows(b, r))
+
+        whole = slice(0, BLOCK)
+        transpose_w(0, 0)
+        transpose_w(0, 1)
+        quantize_w_rows(0, 0)
         bias_chunk(0)
         tables_to_psum()
+        transpose_w(0, 2)
+        quantize_w_rows(0, 1)
+        transpose_w(0, 3)
+        quantize_w_rows(0, 2)
+        quantize_w_rows(0, 3)
+        transpose_x(0)
         transpose_x(1)
         quantize_x(0)
         quantize_x(1)
@@ -310,17 +348,18 @@ def tile_attention_pa_kernel(
         sort_x_words(3)
         for b in range(N_BLOCKS):
             more = b + 1 < N_BLOCKS
+            load_block(b + 3)
             if b == 0:
                 transpose_w(1, 0)
-                us = add_bias(0, [multiply(0, 0)])
+                add_bias(0, 0, multiply(0, 0), whole)
                 transpose_w(1, 1)
                 transpose_x(2)
                 acc = multiply(0, 1)
-                rotate_and_store(0, (0,), us)
-                us = add_bias(0, [acc])
+                rotate_single(0, 0)
+                add_bias(0, 1, acc, whole)
                 transpose_x(3)
                 quantize_x(2)
-                rotate_and_store(0, (1,), us)
+                rotate_single(0, 1)
                 quantize_x(3)
             else:
                 if more:
@@ -328,10 +367,13 @@ def tile_attention_pa_kernel(
                     transpose_w(b + 1, 1)
                     sort_words(b + 1, 3)
                 accs = [multiply(b, 0), multiply(b, 1)]
-                if b == V_BLOCK:
-                    add_bias_and_store_v((0, 1), accs)
-                else:
-                    rotate_and_store(b, (0, 1), add_bias(b, accs))
+                for m in (0, 1):
+                    if b == V_BLOCK:
+                        add_bias_and_store_v(m, accs[m])
+                    else:
+                        add_bias(b, m, accs[m], whole)
+                if b < V_BLOCK:
+                    rotate_first_pair(b)
             if more:
                 transpose_w(b + 1, 2)
                 transpose_w(b + 1, 3)
@@ -342,7 +384,10 @@ def tile_attention_pa_kernel(
             if more:
                 quantize_w(b + 1, 0)
                 quantize_w(b + 1, 1)
-            if b == V_BLOCK:
-                add_bias_and_store_v((2, 3), accs)
-            else:
-                rotate_and_store(b, (2, 3), add_bias(b, accs))
+            for m in (2, 3):
+                if b == V_BLOCK:
+                    add_bias_and_store_v(m, accs[m - 2])
+                else:
+                    add_bias(b, m, accs[m - 2], whole)
+            if b < V_BLOCK:
+                rotate_second_pair(b)

@@ -21,8 +21,6 @@ HEADS = 4
 HALF = 64
 N_BLOCKS = 6
 V_BLOCK = 5
-FIRST_SORTED = 2
-SORTED_ROW_TILES = (1, 2, 3)
 
 
 def tile_attention_pa_kernel(
@@ -130,12 +128,10 @@ def tile_attention_pa_kernel(
 
         sorted_w = {}
 
-        def sort_words(b, r):
-            if FIRST_SORTED <= b < N_BLOCKS and r in SORTED_ROW_TILES:
+        def sort_words(copy, b, r):
+            if b < N_BLOCKS:
                 ro = rop.tile([P, PASSES, 2, P], F32, name="ro")
-                nc.scalar.copy(
-                    out=ro[:], in_=raw_w[(b, r)][:].bitcast(F32).rearrange("p (g w u) -> p g u w", g=PASSES, u=2)
-                )
+                copy(out=ro[:], in_=raw_w[(b, r)][:].bitcast(F32).rearrange("p (g w u) -> p g u w", g=PASSES, u=2))
                 sorted_w[(b, r)] = ro
 
         x_codes = {}
@@ -303,17 +299,12 @@ def tile_attention_pa_kernel(
             add_products(b, (0, 1))
             store(b, (0, 1))
 
-        def rotate_second_pair(b):
-            if b == 0:
-                multiply_by_cos_on_gpsimd(b, 3)
-            multiply_by_cos_on_vector(b, 2)
-            multiply_by_sin(b, 2)
-            add_products(b, (2,))
-            if b > 0:
-                multiply_by_cos_on_vector(b, 3)
-            multiply_by_sin(b, 3)
-            add_products(b, (3,))
-            store(b, (2, 3))
+        def rotate_second_pair_tile(b, m):
+            if not (b == 0 and m == 3):
+                multiply_by_cos_on_vector(b, m)
+            multiply_by_sin(b, m)
+            add_products(b, (m,))
+            store(b, (m,))
 
         def add_bias_and_store_v(m, acc):
             pieces = 2 if m == 3 else 1
@@ -343,15 +334,15 @@ def tile_attention_pa_kernel(
         transpose_x(0)
         transpose_x(1)
         quantize_x(0)
+        sort_words(nc.vector.tensor_copy, 1, 1)
         quantize_x(1)
         sort_x_words(2)
-        sort_x_words(3)
-        for b in range(N_BLOCKS):
-            more = b + 1 < N_BLOCKS
+        for b in range(V_BLOCK):
             load_block(b + 3)
             if b == 0:
                 transpose_w(1, 0)
                 add_bias(0, 0, multiply(0, 0), whole)
+                sort_x_words(3)
                 transpose_w(1, 1)
                 transpose_x(2)
                 acc = multiply(0, 1)
@@ -362,32 +353,32 @@ def tile_attention_pa_kernel(
                 rotate_single(0, 1)
                 quantize_x(3)
             else:
-                if more:
-                    transpose_w(b + 1, 0)
-                    transpose_w(b + 1, 1)
-                    sort_words(b + 1, 3)
+                transpose_w(b + 1, 0)
+                transpose_w(b + 1, 1)
+                sort_words(nc.scalar.copy, b + 1, 3)
                 accs = [multiply(b, 0), multiply(b, 1)]
                 for m in (0, 1):
-                    if b == V_BLOCK:
-                        add_bias_and_store_v(m, accs[m])
-                    else:
-                        add_bias(b, m, accs[m], whole)
-                if b < V_BLOCK:
-                    rotate_first_pair(b)
-            if more:
-                transpose_w(b + 1, 2)
-                transpose_w(b + 1, 3)
-                bias_chunk(b + 1)
-                sort_words(b + 2, 1)
-                sort_words(b + 2, 2)
+                    add_bias(b, m, accs[m], whole)
+                rotate_first_pair(b)
+            transpose_w(b + 1, 2)
+            transpose_w(b + 1, 3)
+            bias_chunk(b + 1)
+            sort_words(nc.scalar.copy, b + 2, 1)
+            sort_words(nc.scalar.copy, b + 2, 2)
             accs = [multiply(b, 2), multiply(b, 3)]
-            if more:
-                quantize_w(b + 1, 0)
-                quantize_w(b + 1, 1)
+            quantize_w(b + 1, 0)
+            quantize_w(b + 1, 1)
             for m in (2, 3):
-                if b == V_BLOCK:
-                    add_bias_and_store_v(m, accs[m - 2])
-                else:
-                    add_bias(b, m, accs[m - 2], whole)
-            if b < V_BLOCK:
-                rotate_second_pair(b)
+                add_bias(b, m, accs[m - 2], whole)
+            if b == 0:
+                multiply_by_cos_on_gpsimd(0, 3)
+            if b + 1 < V_BLOCK:
+                rotate_second_pair_tile(b, 2)
+                rotate_second_pair_tile(b, 3)
+        accs = [multiply(V_BLOCK, 0), multiply(V_BLOCK, 1)]
+        rotate_second_pair_tile(V_BLOCK - 1, 2)
+        add_bias_and_store_v(0, accs[0])
+        rotate_second_pair_tile(V_BLOCK - 1, 3)
+        add_bias_and_store_v(1, accs[1])
+        for m in (2, 3):
+            add_bias_and_store_v(m, multiply(V_BLOCK, m))

@@ -35,13 +35,15 @@ def tile_attention_pa_kernel(
             return k_w[P * r : P * (r + 1), :]
         return v_w[P * r : P * (r + 1), :]
 
-    def out_rows(b, m):
-        rows = slice(P * m, P * (m + 1))
+    def out_rows(b, m, n):
+        rows = slice(P * m, P * (m + n))
         if b < 4:
-            return out_0[0, rows, HEADS * b : HEADS * (b + 1), :].rearrange("s h d -> s (h d)")
-        if b == 4:
-            return out_1[0, rows, :, :].rearrange("s h d -> s (h d)")
-        return out_2[0, rows, :, :].rearrange("s h d -> s (h d)")
+            block = out_0[0, rows, HEADS * b : HEADS * (b + 1), :]
+        elif b == 4:
+            block = out_1[0, rows, :, :]
+        else:
+            block = out_2[0, rows, :, :]
+        return block.rearrange("(m p) h d -> p m (h d)", p=P)
 
     with ExitStack() as ctx:
         const = ctx.enter_context(tc.tile_pool(name="const", bufs=1))
@@ -282,8 +284,8 @@ def tile_attention_pa_kernel(
             nc.gpsimd.tensor_tensor(out=t1, in0=t1, in1=t2, op=ADD)
 
         def store(b, ms):
-            for m in ms:
-                nc.sync.dma_start(out=out_rows(b, m), in_=half_of_pair(by_cos, outp, "t1", b, m))
+            some = slice(ms[0] % 2, ms[0] % 2 + len(ms))
+            nc.sync.dma_start(out=out_rows(b, ms[0], len(ms)), in_=by_cos[(b, ms[0] // 2)][:, some, :])
 
         def rotate_single(b, m):
             multiply_by_cos_on_vector(b, m)
@@ -313,7 +315,7 @@ def tile_attention_pa_kernel(
                 cols = slice(width * i, width * (i + 1))
                 add_bias(V_BLOCK, m, acc, cols)
                 u = half_of_pair(biased, epp, "u", V_BLOCK, m)
-                nc.scalar.dma_start(out=out_rows(V_BLOCK, m)[:, cols], in_=u[:, cols])
+                nc.scalar.dma_start(out=out_rows(V_BLOCK, m, 1)[:, 0, cols], in_=u[:, cols])
 
         def load_block(b):
             if b < N_BLOCKS:

@@ -99,8 +99,8 @@ def tile_attention_pa_kernel(
         cc = const.tile([P, 4, HALF, 2], BF16, name="cc")
         nn = const.tile([P, 4, HALF, 2], BF16, name="nn")
         nc.vector.tensor_copy(out=cc[:], in_=cos_t[:].unsqueeze(3).to_broadcast([P, 4, HALF, 2]))
-        nc.vector.tensor_scalar(out=nn[:, :, :, 0], in0=sin_t[:], scalar1=-1.0, scalar2=None, op0=MULT)
-        nc.vector.tensor_copy(out=nn[:, :, :, 1], in_=sin_t[:])
+        nc.vector.tensor_copy(out=nn[:, :, :, 0], in_=sin_t[:])
+        nc.vector.tensor_scalar(out=nn[:, :, :, 1], in0=sin_t[:], scalar1=-1.0, scalar2=None, op0=MULT)
         ident_b = const.tile([P, P], BF16, name="ident_b")
         make_identity(nc, ident_b[:])
         tabs = tabp.tile([P, 2, 4, P], BF16, name="tabs")
@@ -237,74 +237,68 @@ def tile_attention_pa_kernel(
             return acc
 
         biased = {}
-        by_cos = {}
-        by_sin = {}
+        products = {}
 
-        def half_of_pair(tiles, pool, tag, b, m):
+        def biased_tile(b, m):
             key = (b, m // 2)
-            if key not in tiles:
-                t = pool.tile([P, 2, BLOCK], F32, name=tag)
-                tiles[key] = t
-            return tiles[key][:, m % 2, :]
+            if key not in biased:
+                u = epp.tile([P, 2, BLOCK], F32, name="u")
+                biased[key] = u
+            return biased[key][:, m % 2, :]
+
+        def products_tile(b, m):
+            key = (b, m // 2)
+            if key not in products:
+                t = outp.tile([P, 2, 2, BLOCK], F32, name="t")
+                products[key] = t
+            return products[key][:, m % 2, :, :]
 
         def add_bias(b, m, acc, cols):
-            u = half_of_pair(biased, epp, "u", b, m)
+            u = biased_tile(b, m)
             nc.vector.tensor_tensor(out=u[:, cols], in0=acc[:, cols], in1=bias_bc[b][:, cols], op=ADD)
 
-        def multiply_by_cos(engine, table, b, m):
-            t1 = half_of_pair(by_cos, outp, "t1", b, m)
-            u = half_of_pair(biased, epp, "u", b, m)
-            engine.tensor_tensor(
-                out=t1.rearrange("p (h d) -> p h d", h=HEADS),
-                in0=u.rearrange("p (h d) -> p h d", h=HEADS),
-                in1=table.unsqueeze(1).to_broadcast([P, HEADS, P]),
+        def multiply_by_tables(b, m, first):
+            n = 2 - first
+            nc.vector.tensor_tensor(
+                out=products_tile(b, m)[:, first:, :].rearrange("p i (h d) -> p i h d", h=HEADS),
+                in0=biased_tile(b, m).rearrange("p (h d) -> p h d", h=HEADS).unsqueeze(1).to_broadcast([P, n, HEADS, P]),
+                in1=tabs[:, first:, m, :].unsqueeze(2).to_broadcast([P, n, HEADS, P]),
                 op=MULT,
             )
 
-        def multiply_by_cos_on_vector(b, m):
-            multiply_by_cos(nc.vector, tabs[:, 0, m, :], b, m)
-
         def multiply_by_cos_on_gpsimd(b, m):
-            multiply_by_cos(nc.gpsimd, cc[:, m, :, :].rearrange("p j e -> p (j e)"), b, m)
-
-        def multiply_by_sin(b, m):
-            t2 = half_of_pair(by_sin, epp, "t2", b, m)
-            u = half_of_pair(biased, epp, "u", b, m)
-            nc.vector.tensor_tensor(
-                out=t2.rearrange("p (h j e) -> p h j e", h=HEADS, e=2),
-                in0=u.rearrange("p (h j e) -> p h j e", h=HEADS, e=2)[:, :, :, ::-1],
-                in1=tabs[:, 1, m, :].rearrange("p (j e) -> p j e", e=2).unsqueeze(1).to_broadcast([P, HEADS, HALF, 2]),
+            nc.gpsimd.tensor_tensor(
+                out=products_tile(b, m)[:, 0, :].rearrange("p (h d) -> p h d", h=HEADS),
+                in0=biased_tile(b, m).rearrange("p (h d) -> p h d", h=HEADS),
+                in1=cc[:, m, :, :].rearrange("p j e -> p (j e)").unsqueeze(1).to_broadcast([P, HEADS, P]),
                 op=MULT,
             )
 
         def add_products(b, ms):
             some = slice(ms[0] % 2, ms[0] % 2 + len(ms))
-            t1 = by_cos[(b, ms[0] // 2)][:, some, :]
-            t2 = by_sin[(b, ms[0] // 2)][:, some, :]
-            nc.gpsimd.tensor_tensor(out=t1, in0=t1, in1=t2, op=ADD)
+            t = products[(b, ms[0] // 2)]
+            by_cos = t[:, some, 0, :].rearrange("p m (j e) -> p m j e", e=2)
+            by_sin = t[:, some, 1, :].rearrange("p m (j e) -> p m j e", e=2)
+            nc.gpsimd.tensor_tensor(out=by_cos, in0=by_cos, in1=by_sin[:, :, :, ::-1], op=ADD)
 
         def store(b, ms):
             some = slice(ms[0] % 2, ms[0] % 2 + len(ms))
-            nc.sync.dma_start(out=out_rows(b, ms[0], len(ms)), in_=by_cos[(b, ms[0] // 2)][:, some, :])
+            nc.sync.dma_start(out=out_rows(b, ms[0], len(ms)), in_=products[(b, ms[0] // 2)][:, some, 0, :])
 
         def rotate_single(b, m):
-            multiply_by_cos_on_vector(b, m)
-            multiply_by_sin(b, m)
+            multiply_by_tables(b, m, 0)
             add_products(b, (m,))
             store(b, (m,))
 
         def rotate_first_pair(b):
             multiply_by_cos_on_gpsimd(b, 1)
-            multiply_by_cos_on_vector(b, 0)
-            multiply_by_sin(b, 0)
-            multiply_by_sin(b, 1)
+            multiply_by_tables(b, 0, 0)
+            multiply_by_tables(b, 1, 1)
             add_products(b, (0, 1))
             store(b, (0, 1))
 
         def rotate_second_pair_tile(b, m):
-            if not (b == 0 and m == 3):
-                multiply_by_cos_on_vector(b, m)
-            multiply_by_sin(b, m)
+            multiply_by_tables(b, m, 1 if (b == 0 and m == 3) else 0)
             add_products(b, (m,))
             store(b, (m,))
 
@@ -314,7 +308,7 @@ def tile_attention_pa_kernel(
             for i in range(pieces):
                 cols = slice(width * i, width * (i + 1))
                 add_bias(V_BLOCK, m, acc, cols)
-                u = half_of_pair(biased, epp, "u", V_BLOCK, m)
+                u = biased_tile(V_BLOCK, m)
                 nc.scalar.dma_start(out=out_rows(V_BLOCK, m, 1)[:, 0, cols], in_=u[:, cols])
 
         def load_block(b):

@@ -36,14 +36,13 @@ def tile_attention_pa_kernel(
         return v_w[P * r : P * (r + 1), :]
 
     def out_rows(b, m, n):
-        rows = slice(P * m, P * (m + n))
         if b < 4:
-            block = out_0[0, rows, HEADS * b : HEADS * (b + 1), :]
+            block = out_0[0, :, HEADS * b : HEADS * (b + 1), :]
         elif b == 4:
-            block = out_1[0, rows, :, :]
+            block = out_1[0, :, :, :]
         else:
-            block = out_2[0, rows, :, :]
-        return block.rearrange("(m p) h d -> p m (h d)", p=P)
+            block = out_2[0, :, :, :]
+        return block.rearrange("(p m) h d -> p m (h d)", m=4)[:, m : m + n, :]
 
     with ExitStack() as ctx:
         const = ctx.enter_context(tc.tile_pool(name="const", bufs=1))
@@ -64,12 +63,12 @@ def tile_attention_pa_kernel(
             return t
 
         def x_rows(m):
-            return x[0, P * m : P * (m + 1), :]
+            return x[0, :, :].rearrange("(p m) k -> p m k", m=4)[:, m, :]
 
         cos_t = const.tile([P, 4, HALF], BF16, name="cos_t")
         sin_t = const.tile([P, 4, HALF], BF16, name="sin_t")
-        nc.scalar.dma_start(out=cos_t[:], in_=precomp_freqs_cos.rearrange("(m p) j -> p m j", p=P))
-        nc.scalar.dma_start(out=sin_t[:], in_=precomp_freqs_sin.rearrange("(m p) j -> p m j", p=P))
+        nc.scalar.dma_start(out=cos_t[:], in_=precomp_freqs_cos.rearrange("(p m) j -> p m j", m=4))
+        nc.scalar.dma_start(out=sin_t[:], in_=precomp_freqs_sin.rearrange("(p m) j -> p m j", m=4))
         brow = const.tile([P, BLOCK], BF16, name="brow")
         nc.vector.memset(brow[:].bitcast(F32), 0.0)
         nc.scalar.dma_start(out=brow[0:4, :], in_=q_b.rearrange("(o n) -> o n", o=4))

@@ -345,8 +345,8 @@ def tile_attention_pa_kernel(
                 add_bias(0, 1, acc, whole)
                 transpose_x(3)
                 quantize_x(2)
-                rotate_single(0, 1)
                 quantize_x(3)
+                rotate_single(0, 1)
             else:
                 transpose_w(b + 1, 0)
                 transpose_w(b + 1, 1)

@@ -297,7 +297,7 @@ def tile_attention_pa_kernel(
             store(b, (0, 1))
 
         def rotate_second_pair_tile(b, m):
-            multiply_by_tables(b, m, 1 if (b == 0 and m == 3) else 0)
+            multiply_by_tables(b, m, 0)
             add_products(b, (m,))
             store(b, (m,))
 
@@ -365,8 +365,6 @@ def tile_attention_pa_kernel(
             quantize_w(b + 1, 1)
             for m in (2, 3):
                 add_bias(b, m, accs[m - 2], whole)
-            if b == 0:
-                multiply_by_cos_on_gpsimd(0, 3)
             if b + 1 < V_BLOCK:
                 rotate_second_pair_tile(b, 2)
                 rotate_second_pair_tile(b, 3)

from contextlib import ExitStack

import concourse.mybir as mybir
from concourse.masks import make_identity

FLOPS = 2 * 512 * 2048 * 3072

F32 = mybir.dt.float32
BF16 = mybir.dt.bfloat16
U32 = mybir.dt.uint32
U8 = mybir.dt.uint8
FP8X4 = mybir.dt.float8_e5m2_x4
ADD = mybir.AluOpType.add
MULT = mybir.AluOpType.mult

P = 128
HID = 2048
PASSES = 4
BLOCK = 512
HEADS = 4
HALF = 64
N_BLOCKS = 6
V_BLOCK = 5


def tile_attention_pa_kernel(
    tc, x, precomp_freqs_cos, precomp_freqs_sin, q_w, q_b, k_w, k_b, v_w, v_b, out_0, out_1, out_2
):
    nc = tc.nc

    def w_rows(b, r):
        if b < 4:
            return q_w[BLOCK * b + P * r : BLOCK * b + P * (r + 1), :]
        if b == 4:
            return k_w[P * r : P * (r + 1), :]
        return v_w[P * r : P * (r + 1), :]

    def out_rows(b, m, n):
        if b < 4:
            block = out_0[0, :, HEADS * b : HEADS * (b + 1), :]
        elif b == 4:
            block = out_1[0, :, :, :]
        else:
            block = out_2[0, :, :, :]
        return block.rearrange("(p m) h d -> p m (h d)", m=4)[:, m : m + n, :]

    with ExitStack() as ctx:
        const = ctx.enter_context(tc.tile_pool(name="const", bufs=1))
        rawp = ctx.enter_context(tc.tile_pool(name="rawp", bufs=16))
        grpp = ctx.enter_context(tc.tile_pool(name="grpp", bufs=2))
        codep = ctx.enter_context(tc.tile_pool(name="codep", bufs=2))
        epp = ctx.enter_context(tc.tile_pool(name="epp", bufs=2))
        outp = ctx.enter_context(tc.tile_pool(name="outp", bufs=3))
        rop = ctx.enter_context(tc.tile_pool(name="rop", bufs=6))
        tpp = ctx.enter_context(tc.psum_pool(name="tpp", bufs=4))
        accp = ctx.enter_context(tc.psum_pool(name="accp", bufs=3))
        tabp = ctx.enter_context(tc.psum_pool(name="tabp", bufs=1))
        ctx.enter_context(tc.manual_schedule())

        def load(rows):
            t = rawp.tile([P, HID], BF16, name="raw")
            nc.sync.dma_start(out=t[:], in_=rows)
            return t

        def x_rows(m):
            return x[0, :, :].rearrange("(p m) k -> p m k", m=4)[:, m, :]

        cos_t = const.tile([P, 4, HALF], BF16, name="cos_t")
        sin_t = const.tile([P, 4, HALF], BF16, name="sin_t")
        nc.scalar.dma_start(out=cos_t[:], in_=precomp_freqs_cos.rearrange("(p m) j -> p m j", m=4))
        nc.scalar.dma_start(out=sin_t[:], in_=precomp_freqs_sin.rearrange("(p m) j -> p m j", m=4))
        brow = const.tile([P, BLOCK], BF16, name="brow")
        nc.vector.memset(brow[:].bitcast(F32), 0.0)
        nc.scalar.dma_start(out=brow[0:4, :], in_=q_b.rearrange("(o n) -> o n", o=4))
        nc.scalar.dma_start(out=brow[4:5, :], in_=k_b.rearrange("(o n) -> o n", o=1))
        nc.scalar.dma_start(out=brow[5:6, :], in_=v_b.rearrange("(o n) -> o n", o=1))
        warm = const.tile([P, 2], F32, name="warm")
        nc.vector.memset(warm[:, 0:1], 0.0)
        nc.scalar.copy(out=warm[:, 1:2], in_=warm[:, 0:1])

        raw_w = {}
        raw_x = {}
        for r in range(4):
            raw_w[(0, r)] = load(w_rows(0, r))
        raw_x[0] = load(x_rows(0))
        raw_x[1] = load(x_rows(1))
        raw_w[(1, 0)] = load(w_rows(1, 0))
        raw_w[(1, 1)] = load(w_rows(1, 1))
        raw_x[2] = load(x_rows(2))
        raw_x[3] = load(x_rows(3))
        raw_w[(1, 2)] = load(w_rows(1, 2))
        raw_w[(1, 3)] = load(w_rows(1, 3))
        for r in range(4):
            raw_w[(2, r)] = load(w_rows(2, r))

        ident = const.tile([P, P], F32, name="ident")
        make_identity(nc, ident[:])
        cc = const.tile([P, 4, HALF, 2], BF16, name="cc")
        nn = const.tile([P, 4, HALF, 2], BF16, name="nn")
        nc.vector.tensor_copy(out=cc[:], in_=cos_t[:].unsqueeze(3).to_broadcast([P, 4, HALF, 2]))
        nc.vector.tensor_copy(out=nn[:, :, :, 0], in_=sin_t[:])
        nc.vector.tensor_scalar(out=nn[:, :, :, 1], in0=sin_t[:], scalar1=-1.0, scalar2=None, op0=MULT)
        ident_b = const.tile([P, P], BF16, name="ident_b")
        make_identity(nc, ident_b[:])
        tabs = tabp.tile([P, 2, 4, P], BF16, name="tabs")

        def tables_to_psum():
            for m in range(4):
                for i, t in enumerate((cc, nn)):
                    nc.tensor.matmul(
                        out=tabs[:, i, m, :],
                        lhsT=ident_b[:],
                        rhs=t[:, m, :, :].rearrange("p j e -> p (j e)"),
                        start=True,
                        stop=True,
                    )

        def transpose_rows(columns, dst):
            for h in range(2):
                tp = tpp.tile([P, 2, 2, P], F32, name="tp")
                for gg in range(2):
                    for u in range(2):
                        nc.tensor.transpose(tp[:, gg, u, :], columns(2 * h + gg, u), ident[:])
                nc.scalar.copy(out=dst(h), in_=tp[:].rearrange("p g u r -> p g r u"))

        def every_second_word(raw_t):
            words = raw_t[:].bitcast(F32)
            return lambda g, u: words[:, 256 * g + u : 256 * (g + 1) : 2]

        sorted_w = {}

        def sort_words(copy, b, r):
            if b < N_BLOCKS:
                ro = rop.tile([P, PASSES, 2, P], F32, name="ro")
                copy(out=ro[:], in_=raw_w[(b, r)][:].bitcast(F32).rearrange("p (g w u) -> p g u w", g=PASSES, u=2))
                sorted_w[(b, r)] = ro

        x_codes = {}
        x_scales = {}

        sorted_x = {}

        def sort_x_words(m):
            ro = rop.tile([P, PASSES, 2, P], F32, name="rox")
            nc.vector.tensor_copy(
                out=ro[:], in_=raw_x[m][:].bitcast(F32).rearrange("p (g w u) -> p g u w", g=PASSES, u=2)
            )
            sorted_x[m] = ro

        grp_x = {}

        def transpose_x(m):
            grp = grpp.tile([P, PASSES, P, 4], BF16, name="grpx", align_bytes=64)
            gw = grp[:].bitcast(F32)
            if m in sorted_x:
                ro = sorted_x[m]
                columns = lambda g, u: ro[:, g, u, :]
            else:
                columns = every_second_word(raw_x[m])
            transpose_rows(columns, lambda h: gw[:, 2 * h : 2 * h + 2, :, :])
            grp_x[m] = grp

        def quantize_x(m):
            xc = const.tile([P, PASSES, P], U32, name="xc%d" % m, align_bytes=64)
            xs = const.tile([P, PASSES, P], U8, name="xs%d" % m, align_bytes=64)
            nc.vector.quantize_mx(
                out=xc[:].rearrange("p g c -> p (g c)").bitcast(FP8X4),
                scales=xs[:].rearrange("p g c -> p (g c)"),
                in_=grp_x[m][:].rearrange("p g c t -> p (g c t)"),
            )
            x_codes[m] = xc
            x_scales[m] = xs

        grp_w = {}
        w_codes = {}
        w_scales = {}

        def transpose_w(b, r):
            if r == 0:
                grp_w[b] = grpp.tile([P, PASSES, BLOCK, 4], BF16, name="grpw", align_bytes=64)
            gw = grp_w[b][:].bitcast(F32)
            if (b, r) in sorted_w:
                ro = sorted_w[(b, r)]
                columns = lambda g, u: ro[:, g, u, :]
            else:
                columns = every_second_word(raw_w[(b, r)])
            transpose_rows(columns, lambda h: gw[:, 2 * h : 2 * h + 2, P * r : P * (r + 1), :])

        def w_code_tiles(b):
            w_codes[b] = codep.tile([P, PASSES, BLOCK], U32, name="wc", align_bytes=64)
            w_scales[b] = codep.tile([P, PASSES, BLOCK], U8, name="ws", align_bytes=64)

        def quantize_w_rows(b, r):
            if r == 0:
                w_code_tiles(b)
            cols = slice(P * r, P * (r + 1))
            for g in range(PASSES):
                nc.vector.quantize_mx(
                    out=w_codes[b][:, g, cols].bitcast(FP8X4),
                    scales=w_scales[b][:, g, cols],
                    in_=grp_w[b][:, g, cols, :].rearrange("p c t -> p (c t)"),
                )

        def quantize_w(b, h):
            if h == 0:
                w_code_tiles(b)
            two = slice(2 * h, 2 * h + 2)
            nc.vector.quantize_mx(
                out=w_codes[b][:, two, :].rearrange("p g c -> p (g c)").bitcast(FP8X4),
                scales=w_scales[b][:, two, :].rearrange("p g c -> p (g c)"),
                in_=grp_w[b][:, two, :, :].rearrange("p g c t -> p (g c t)"),
            )

        bias_bc = {}

        def bias_chunk(b):
            ps = tpp.tile([P, BLOCK], F32, name="tp")
            nc.tensor.matmul(
                out=ps[:], lhsT=ident_b[:, b : b + 1].to_broadcast([P, P]), rhs=brow[:], start=True, stop=True
            )
            bias_bc[b] = const.tile([P, BLOCK], F32, name="bias%d" % b)
            nc.scalar.copy(out=bias_bc[b][:], in_=ps[:])

        def multiply(b, m):
            acc = accp.tile([P, BLOCK], F32, name="acc")
            for g in range(PASSES):
                nc.tensor.matmul_mx(
                    out=acc[:],
                    lhsT=x_codes[m][:, g, :].bitcast(FP8X4),
                    lhsT_scale=x_scales[m][:, g, :],
                    rhs=w_codes[b][:, g, :].bitcast(FP8X4),
                    rhs_scale=w_scales[b][:, g, :],
                    start=(g == 0),
                    stop=(g == PASSES - 1),
                )
            return acc

        biased = {}
        products = {}

        def biased_tile(b, m):
            key = (b, m // 2)
            if key not in biased:
                u = epp.tile([P, 2, BLOCK], F32, name="u")
                biased[key] = u
            return biased[key][:, m % 2, :]

        def products_tile(b, m):
            key = (b, m // 2)
            if key not in products:
                t = outp.tile([P, 2, 2, BLOCK], F32, name="t")
                products[key] = t
            return products[key][:, m % 2, :, :]

        def add_bias(b, m, acc, cols):
            u = biased_tile(b, m)
            nc.vector.tensor_tensor(out=u[:, cols], in0=acc[:, cols], in1=bias_bc[b][:, cols], op=ADD)

        def multiply_by_tables(b, m, first):
            n = 2 - first
            nc.vector.tensor_tensor(
                out=products_tile(b, m)[:, first:, :].rearrange("p i (h d) -> p i h d", h=HEADS),
                in0=biased_tile(b, m).rearrange("p (h d) -> p h d", h=HEADS).unsqueeze(1).to_broadcast([P, n, HEADS, P]),
                in1=tabs[:, first:, m, :].unsqueeze(2).to_broadcast([P, n, HEADS, P]),
                op=MULT,
            )

        def multiply_by_cos_on_gpsimd(b, m):
            nc.gpsimd.tensor_tensor(
                out=products_tile(b, m)[:, 0, :].rearrange("p (h d) -> p h d", h=HEADS),
                in0=biased_tile(b, m).rearrange("p (h d) -> p h d", h=HEADS),
                in1=cc[:, m, :, :].rearrange("p j e -> p (j e)").unsqueeze(1).to_broadcast([P, HEADS, P]),
                op=MULT,
            )

        def add_products(b, ms):
            some = slice(ms[0] % 2, ms[0] % 2 + len(ms))
            t = products[(b, ms[0] // 2)]
            by_cos = t[:, some, 0, :].rearrange("p m (j e) -> p m j e", e=2)
            by_sin = t[:, some, 1, :].rearrange("p m (j e) -> p m j e", e=2)
            nc.gpsimd.tensor_tensor(out=by_cos, in0=by_cos, in1=by_sin[:, :, :, ::-1], op=ADD)

        def store(b, ms):
            some = slice(ms[0] % 2, ms[0] % 2 + len(ms))
            nc.sync.dma_start(out=out_rows(b, ms[0], len(ms)), in_=products[(b, ms[0] // 2)][:, some, 0, :])

        def rotate_single(b, m):
            multiply_by_tables(b, m, 0)
            add_products(b, (m,))
            store(b, (m,))

        def rotate_first_pair(b):
            multiply_by_cos_on_gpsimd(b, 1)
            multiply_by_tables(b, 0, 0)
            multiply_by_tables(b, 1, 1)
            add_products(b, (0, 1))
            store(b, (0, 1))

        def rotate_second_pair_tile(b, m):
            multiply_by_tables(b, m, 0)
            add_products(b, (m,))
            store(b, (m,))

        def add_bias_and_store_v(m, acc):
            pieces = 2 if m == 3 else 1
            width = BLOCK // pieces
            for i in range(pieces):
                cols = slice(width * i, width * (i + 1))
                add_bias(V_BLOCK, m, acc, cols)
                u = biased_tile(V_BLOCK, m)
                nc.scalar.dma_start(out=out_rows(V_BLOCK, m, 1)[:, 0, cols], in_=u[:, cols])

        def load_block(b):
            if b < N_BLOCKS:
                for r in range(4):
                    raw_w[(b, r)] = load(w_rows(b, r))

        whole = slice(0, BLOCK)
        transpose_w(0, 0)
        transpose_w(0, 1)
        quantize_w_rows(0, 0)
        bias_chunk(0)
        tables_to_psum()
        transpose_w(0, 2)
        quantize_w_rows(0, 1)
        transpose_w(0, 3)
        quantize_w_rows(0, 2)
        quantize_w_rows(0, 3)
        transpose_x(0)
        transpose_x(1)
        quantize_x(0)
        sort_words(nc.vector.tensor_copy, 1, 1)
        quantize_x(1)
        sort_x_words(2)
        for b in range(V_BLOCK):
            load_block(b + 3)
            if b == 0:
                transpose_w(1, 0)
                add_bias(0, 0, multiply(0, 0), whole)
                sort_x_words(3)
                transpose_w(1, 1)
                transpose_x(2)
                acc = multiply(0, 1)
                rotate_single(0, 0)
                add_bias(0, 1, acc, whole)
                transpose_x(3)
                quantize_x(2)
                quantize_x(3)
                rotate_single(0, 1)
            else:
                transpose_w(b + 1, 0)
                transpose_w(b + 1, 1)
                sort_words(nc.scalar.copy, b + 1, 3)
                accs = [multiply(b, 0), multiply(b, 1)]
                for m in (0, 1):
                    add_bias(b, m, accs[m], whole)
                rotate_first_pair(b)
            transpose_w(b + 1, 2)
            transpose_w(b + 1, 3)
            bias_chunk(b + 1)
            sort_words(nc.scalar.copy, b + 2, 1)
            sort_words(nc.scalar.copy, b + 2, 2)
            accs = [multiply(b, 2), multiply(b, 3)]
            quantize_w(b + 1, 0)
            quantize_w(b + 1, 1)
            for m in (2, 3):
                add_bias(b, m, accs[m - 2], whole)
            if b + 1 < V_BLOCK:
                rotate_second_pair_tile(b, 2)
                rotate_second_pair_tile(b, 3)
        accs = [multiply(V_BLOCK, 0), multiply(V_BLOCK, 1)]
        rotate_second_pair_tile(V_BLOCK - 1, 2)
        add_bias_and_store_v(0, accs[0])
        rotate_second_pair_tile(V_BLOCK - 1, 3)
        add_bias_and_store_v(1, accs[1])
        for m in (2, 3):
            add_bias_and_store_v(m, multiply(V_BLOCK, m))
